import numpy as np
import ml_dtypes


def mxq(x, axis, fmt="e4m3"):
    dtype, down = {"e4m3": (ml_dtypes.float8_e4m3fn, 7), "e5m2": (ml_dtypes.float8_e5m2, 14)}[fmt]
    v = np.moveaxis(np.asarray(x, np.float32).astype(ml_dtypes.bfloat16).astype(np.float64), axis, -1)
    blocks = v.reshape(v.shape[:-1] + (-1, 32))
    amax = np.abs(blocks).max(-1, keepdims=True)
    byte = np.maximum(np.where(amax > 0, np.frexp(amax)[1] - 1 + 127, 0) - down, 1)
    scale = np.exp2(byte - 127.0)
    codes = (blocks / scale).astype(np.float32).astype(dtype).astype(np.float64)
    return np.moveaxis((codes * scale).reshape(v.shape), -1, axis)


WIDE = False


def mx_kscale(k):
    if not WIDE:
        return np.ones(k)
    levels = np.array([10, -10, 5, -5, 0])
    a = np.random.permutation(np.resize(levels, k // 512 * 4)).reshape(k // 512, 4)
    idx = np.arange(k)
    return np.exp2(a[idx // 512, idx % 128 // 32])


BF16 = ml_dtypes.bfloat16


def bf(x):
    return np.asarray(x, np.float32).astype(BF16)


def f64(x):
    return np.asarray(x).astype(np.float64)


E2M1 = np.array([0.0, 0.5, 1.0, 1.5, 2.0, 3.0, 4.0, 6.0, -0.0, -0.5, -1.0, -1.5, -2.0, -3.0, -4.0, -6.0])


def pack_weight(w, fmt):
    k, n = w.shape
    w = f64(bf(w)).reshape(k // 32, 32, n)
    amax = np.abs(w).max(1)
    if fmt == "e4m3":
        byte = np.frexp(amax)[1] - 1 + 127 - 7
    else:
        mant, ex = np.frexp(amax / 6.0)
        byte = np.where(mant > 0.5, ex, ex - 1) + 127
    byte = np.clip(np.where(amax > 0, byte, 1), 1, 254)
    scaled = (w * np.exp2(127.0 - byte)[:, None, :]).reshape(k, n).astype(np.float32)
    by_word = np.ascontiguousarray(scaled.reshape(k // 512, 128, 4, n).transpose(0, 1, 3, 2))
    if fmt == "e4m3":
        words = by_word.astype(ml_dtypes.float8_e4m3fn).view(np.uint8)
    else:
        c = by_word.astype(ml_dtypes.float4_e2m1fn).view(np.uint8) & 0xF
        words = c[..., 0::2] | (c[..., 1::2] << 4)
    return np.ascontiguousarray(words), np.ascontiguousarray(byte.astype(np.uint8).reshape(k // 512, 16, n))


def unpack_weight(words, scales, fmt):
    g, p, n, _ = words.shape
    if fmt == "e4m3":
        vals = np.ascontiguousarray(words).view(ml_dtypes.float8_e4m3fn).astype(np.float64)
    else:
        nib = np.empty((g, p, n, 4), np.uint8)
        nib[..., 0::2] = words & 0xF
        nib[..., 1::2] = words >> 4
        vals = E2M1[nib]
    vals = vals * np.repeat(np.exp2(scales.astype(np.float64) - 127.0), 8, axis=1)[..., None]
    return vals.transpose(0, 1, 3, 2).reshape(g * 512, n)

def pack4(w):
    words, scales = pack_weight(w, "e2m1")
    return words.reshape(words.shape[0], 128, -1), scales


def unpack4(words, scales):
    return unpack_weight(words.reshape(words.shape[0], 128, -1, 2), scales, "e2m1")


B, S, D_MODEL, N_HEADS, QK_ROPE, QK_NOPE, KV_LORA, V_DIM = 4, 2048, 1024, 2, 32, 32, 512, 128
QK_DIM = QK_ROPE + QK_NOPE
ROPE_BASE = 10000.0


def apply_rope(r):
    freqs = 1.0 / (ROPE_BASE ** (np.arange(0, QK_ROPE, 2) / QK_ROPE))
    t = np.arange(S)[:, None] * freqs[None, :]
    cos = np.cos(t)[None, :, None, :]
    sin = np.sin(t)[None, :, None, :]
    r1 = r[..., 0::2]
    r2 = r[..., 1::2]
    return np.stack([r1 * cos - r2 * sin, r2 * cos + r1 * sin], axis=-1).reshape(r.shape)


def setup_inputs():
    s = mx_kscale(D_MODEL)
    x = bf(np.random.standard_normal((B, S, D_MODEL)) * s)
    words, scales = pack4(np.random.standard_normal((D_MODEL, N_HEADS * QK_DIM)) / np.sqrt(D_MODEL) / s[:, None])
    return {"x": x, "Wq_words": words, "Wq_scales": scales}


def reference(x, Wq_words, Wq_scales):
    q = (mxq(f64(x), 2, "e4m3") @ unpack4(Wq_words, Wq_scales)).reshape(B, S, N_HEADS, QK_DIM)
    q_nope, q_rope = q[..., :QK_NOPE], q[..., QK_NOPE:]
    return np.concatenate([q_nope, apply_rope(q_rope)], axis=-1)

@@ -1,0 +1,255 @@
+import math
+from contextlib import ExitStack
+
+import concourse.mybir as mybir
+from concourse.masks import make_identity
+
+F32 = mybir.dt.float32
+BF16 = mybir.dt.bfloat16
+I32 = mybir.dt.int32
+U32 = mybir.dt.uint32
+U8 = mybir.dt.uint8
+FP8X4 = mybir.dt.float8_e4m3fn_x4
+FP4X4 = mybir.dt.float4_e2m1fn_x4
+ALU = mybir.AluOpType
+SIN = mybir.ActivationFunctionType.Sin
+
+P = 128
+BATCH, SEQ, K = 4, 2048, 1024
+HEADS, HEAD_DIM, ROPE_DIM = 2, 64, 32
+NOPE_DIM = HEAD_DIM - ROPE_DIM
+PAIRS = ROPE_DIM // 2
+N_OUT = HEADS * HEAD_DIM
+ROPE_BASE = 10000.0
+
+K_PASS = 4 * P
+PASSES = K // K_PASS
+WORDS_PER_PASS = K_PASS // 2
+
+ROWS = SEQ // P
+GROUP = 4
+GROUPS_PER_BATCH = ROWS // GROUP
+N_GROUPS = BATCH * GROUPS_PER_BATCH
+FINE_GROUPS = 4
+QUANT_TILES = 2
+
+ROUND_MAGIC = 1.5 * 2.0**23
+
+FLOPS = 2 * BATCH * SEQ * K * N_OUT
+
+
+def keep_bits(value, bits):
+    if value == 0.0:
+        return 0.0
+    unit = 1.0
+    while abs(value) / unit >= 2.0**bits:
+        unit *= 2.0
+    while abs(value) / unit < 2.0 ** (bits - 1):
+        unit /= 2.0
+    return round(value / unit) * unit
+
+
+def rope_half_turns(nc, keep):
+    table = [P, ROWS, PAIRS]
+
+    rate = keep.tile([P, 2, PAIRS], F32)
+    for i in range(PAIRS):
+        exact = ROPE_BASE ** (-2.0 * i / ROPE_DIM) / math.pi
+        high = keep_bits(exact, 24)
+        nc.vector.memset(rate[:, 0, i : i + 1], high)
+        nc.vector.memset(rate[:, 1, i : i + 1], keep_bits(exact - high, 24))
+
+    position_int = keep.tile([P, ROWS], I32)
+    nc.gpsimd.iota(position_int[:], pattern=[[1, ROWS]], base=0, channel_multiplier=ROWS)
+    position = keep.tile([P, ROWS], F32)
+    nc.vector.tensor_copy(out=position[:], in_=position_int[:])
+    position_all_pairs = position[:].unsqueeze(2).to_broadcast(table)
+
+    turns = keep.tile(table, F32)
+    nc.vector.tensor_tensor(
+        out=turns[:],
+        in0=position_all_pairs,
+        in1=rate[:, 0, :].unsqueeze(1).to_broadcast(table),
+        op=ALU.mult,
+    )
+    turns_rest = keep.tile(table, F32)
+    nc.vector.tensor_tensor(
+        out=turns_rest[:],
+        in0=position_all_pairs,
+        in1=rate[:, 1, :].unsqueeze(1).to_broadcast(table),
+        op=ALU.mult,
+    )
+    rounded = keep.tile(table, F32)
+    nc.vector.tensor_scalar(
+        out=rounded[:], in0=turns[:], scalar1=ROUND_MAGIC, scalar2=None, op0=ALU.add
+    )
+    odd = keep.tile(table, I32)
+    nc.vector.tensor_scalar(
+        out=odd[:], in0=rounded[:].bitcast(I32), scalar1=1, scalar2=None, op0=ALU.bitwise_and
+    )
+    minus_f = keep.tile(table, F32)
+    nc.vector.scalar_tensor_tensor(
+        out=minus_f[:],
+        in0=rounded[:],
+        scalar=ROUND_MAGIC,
+        in1=turns[:],
+        op0=ALU.subtract,
+        op1=ALU.subtract,
+    )
+    sign = keep.tile(table, F32)
+    nc.vector.tensor_scalar(
+        out=sign[:], in0=odd[:], scalar1=-2.0, scalar2=1.0, op0=ALU.mult, op1=ALU.add
+    )
+    f = keep.tile(table, F32)
+    nc.vector.tensor_tensor(out=f[:], in0=turns_rest[:], in1=minus_f[:], op=ALU.subtract)
+    minus_abs_f = keep.tile(table, F32)
+    nc.vector.scalar_tensor_tensor(
+        out=minus_abs_f[:], in0=f[:], scalar=-1.0, in1=f[:], op0=ALU.mult, op1=ALU.min
+    )
+    sin_turns = keep.tile(table, F32)
+    nc.vector.tensor_tensor(out=sin_turns[:], in0=f[:], in1=sign[:], op=ALU.mult)
+    cos_turns = keep.tile(table, F32)
+    nc.vector.scalar_tensor_tensor(
+        out=cos_turns[:], in0=minus_abs_f[:], scalar=0.5, in1=sign[:], op0=ALU.add, op1=ALU.mult
+    )
+    return sin_turns, cos_turns
+
+
+def tile_multiheadlatentattention_pb_t_kernel(tc, x, Wq_words, Wq_scales, out):
+    nc = tc.nc
+    x_rows = x.rearrange("b (p j) k -> b p j k", j=ROWS)
+    out_rows = out.rearrange("b (p j) h d -> b p j h d", j=ROWS)
+
+    with ExitStack() as ctx:
+        keep = ctx.enter_context(tc.tile_pool(name="keep", bufs=1))
+        x_pool = ctx.enter_context(tc.tile_pool(name="x", bufs=N_GROUPS))
+        q_pool = ctx.enter_context(tc.tile_pool(name="q", bufs=N_GROUPS))
+        mx_pool = ctx.enter_context(tc.tile_pool(name="mx", bufs=3))
+        cross_pool = ctx.enter_context(tc.tile_pool(name="cross", bufs=2))
+        xt_pool = ctx.enter_context(tc.psum_pool(name="xt", bufs=6))
+        acc_pool = ctx.enter_context(tc.psum_pool(name="acc", bufs=2))
+        ctx.enter_context(tc.manual_schedule())
+
+        w_planes = keep.tile([P, PASSES, N_OUT], U8, align_bytes=64)
+        nc.vector.memset(w_planes[:].bitcast(I32), 0)
+        sin_warm = keep.tile([P, 1], F32)
+        nc.vector.memset(sin_warm[:], 0.0)
+        identity = keep.tile([P, P], F32)
+        make_identity(nc, identity[:])
+
+        w_words = keep.tile([P, PASSES, 2 * N_OUT], U8, align_bytes=64)
+        nc.sync.dma_start(
+            out=w_words[:].bitcast(I32), in_=Wq_words.rearrange("g p b -> p g b").bitcast(I32)
+        )
+        for quadrant in range(4):
+            nc.sync.dma_start(
+                out=w_planes[32 * quadrant : 32 * quadrant + 4].bitcast(I32),
+                in_=Wq_scales[:, 4 * quadrant : 4 * quadrant + 4, :]
+                .rearrange("g r n -> r g n")
+                .bitcast(I32),
+            )
+        x_tiles = []
+        for group in range(N_GROUPS):
+            x_sb = x_pool.tile([P, GROUP, K], BF16)
+            x_tiles.append(x_sb)
+            batch, first_row = divmod(group * GROUP, ROWS)
+            if group < FINE_GROUPS:
+                for t in range(GROUP):
+                    nc.sync.dma_start(out=x_sb[:, t, :], in_=x_rows[batch, :, first_row + t, :])
+            else:
+                nc.sync.dma_start(
+                    out=x_sb[:], in_=x_rows[batch, :, first_row : first_row + GROUP, :]
+                )
+
+        nc.scalar.activation(out=sin_warm[:], in_=sin_warm[:], func=SIN)
+
+        sin_turns, cos_turns = rope_half_turns(nc, keep)
+        cos_full = keep.tile([P, ROWS, HEAD_DIM], F32)
+        nc.gpsimd.memset(cos_full[:, :, 0:NOPE_DIM], 1.0)
+
+        quantised = {}
+
+        def regroup_and_quantise(group):
+            x_sb = x_tiles[group]
+            grouped = mx_pool.tile([P, GROUP, PASSES, P, 2], F32, align_bytes=64)
+            codes = mx_pool.tile([P, GROUP, PASSES, P], U32, align_bytes=64)
+            planes = mx_pool.tile([P, GROUP, PASSES, P], U8, align_bytes=64)
+            quantised[group] = (codes, planes)
+            for t in range(GROUP):
+                words = x_sb[:, t, :].bitcast(F32)
+                xt = xt_pool.tile([P, PASSES, 2, P], F32)
+                for g in range(PASSES):
+                    for u in range(2):
+                        nc.tensor.transpose(
+                            xt[:, g, u, :],
+                            words[:, WORDS_PER_PASS * g + u : WORDS_PER_PASS * (g + 1) : 2],
+                            identity[:],
+                        )
+                nc.scalar.copy(out=grouped[:, t], in_=xt[:].rearrange("p g u n -> p g n u"))
+                if (t + 1) % QUANT_TILES == 0:
+                    done = slice(t + 1 - QUANT_TILES, t + 1)
+                    nc.vector.quantize_mx(
+                        out=codes[:, done].rearrange("p t g n -> p (t g n)").bitcast(FP8X4),
+                        scales=planes[:, done].rearrange("p t g n -> p (t g n)"),
+                        in_=grouped[:, done].rearrange("p t g n u -> p (t g n u)").bitcast(BF16),
+                    )
+
+        def project_and_rotate(group):
+            codes, planes = quantised[group]
+            batch, first_row = divmod(group * GROUP, ROWS)
+            rows = slice(first_row, first_row + GROUP)
+            acc = acc_pool.tile([P, GROUP, HEADS, HEAD_DIM], F32)
+            for t in range(GROUP):
+                for g in range(PASSES):
+                    nc.tensor.matmul_mx(
+                        out=acc[:, t].rearrange("p h d -> p (h d)"),
+                        lhsT=codes[:, t, g, :].bitcast(FP8X4),
+                        lhsT_scale=planes[:, t, g, :],
+                        rhs=w_words[:, g, :].bitcast(FP4X4),
+                        rhs_scale=w_planes[:, g, :],
+                        start=(g == 0),
+                        stop=(g == PASSES - 1),
+                    )
+            q_sb = q_pool.tile([P, GROUP, HEADS, HEAD_DIM], F32)
+            nc.vector.tensor_tensor(
+                out=q_sb[:],
+                in0=acc[:],
+                in1=cos_full[:, rows, :].unsqueeze(2).to_broadcast([P, GROUP, HEADS, HEAD_DIM]),
+                op=ALU.mult,
+            )
+            pairs = acc[:, :, :, NOPE_DIM:HEAD_DIM].rearrange("p t h (i e) -> p t h i e", e=2)
+            cross = cross_pool.tile([P, 2, GROUP, HEADS, PAIRS], F32)
+            for place in range(2):
+                nc.vector.tensor_tensor(
+                    out=cross[:, place],
+                    in0=pairs[:, :, :, :, 1 - place],
+                    in1=sin_signed[:, place, rows, :]
+                    .unsqueeze(2)
+                    .to_broadcast([P, GROUP, HEADS, PAIRS]),
+                    op=ALU.mult,
+                )
+            rotated = q_sb[:, :, :, NOPE_DIM:HEAD_DIM].rearrange("p t h (i e) -> p t h i e", e=2)
+            nc.vector.tensor_tensor(
+                out=rotated,
+                in0=rotated,
+                in1=cross[:].rearrange("p e t h i -> p t h i e"),
+                op=ALU.add,
+            )
+            nc.sync.dma_start(out=out_rows[batch, :, rows], in_=q_sb[:])
+
+        regroup_and_quantise(0)
+
+        sin_signed = keep.tile([P, 2, ROWS, PAIRS], F32)
+        nc.scalar.activation(out=sin_signed[:, 0], in_=sin_turns[:], func=SIN, scale=-math.pi)
+        nc.scalar.activation(out=sin_signed[:, 1], in_=sin_turns[:], func=SIN, scale=math.pi)
+        nc.scalar.activation(
+            out=cos_full[:, :, NOPE_DIM:HEAD_DIM].rearrange("p j (i e) -> p j i e", e=2),
+            in_=cos_turns[:].unsqueeze(3).to_broadcast([P, ROWS, PAIRS, 2]),
+            func=SIN,
+            scale=math.pi,
+        )
+
+        for group in range(1, N_GROUPS):
+            regroup_and_quantise(group)
+            project_and_rotate(group - 1)
+        project_and_rotate(N_GROUPS - 1)

@@ -30,7 +30,7 @@ ROWS = SEQ // P
 GROUP = 4
 GROUPS_PER_BATCH = ROWS // GROUP
 N_GROUPS = BATCH * GROUPS_PER_BATCH
-FINE_GROUPS = 4
+FINE_GROUPS = 6
 QUANT_TILES = 2
 
 ROUND_MAGIC = 1.5 * 2.0**23
@@ -138,18 +138,23 @@ def tile_multiheadlatentattention_pb_t_kernel(tc, x, Wq_words, Wq_scales, out):
         make_identity(nc, identity[:])
 
         w_words = keep.tile([P, PASSES, 2 * N_OUT], U8, align_bytes=64)
-        nc.sync.dma_start(
-            out=w_words[:].bitcast(I32), in_=Wq_words.rearrange("g p b -> p g b").bitcast(I32)
-        )
-        for quadrant in range(4):
+
+        def load_weight():
             nc.sync.dma_start(
-                out=w_planes[32 * quadrant : 32 * quadrant + 4].bitcast(I32),
-                in_=Wq_scales[:, 4 * quadrant : 4 * quadrant + 4, :]
-                .rearrange("g r n -> r g n")
-                .bitcast(I32),
+                out=w_words[:].bitcast(I32), in_=Wq_words.rearrange("g p b -> p g b").bitcast(I32)
             )
+            for quadrant in range(4):
+                nc.sync.dma_start(
+                    out=w_planes[32 * quadrant : 32 * quadrant + 4].bitcast(I32),
+                    in_=Wq_scales[:, 4 * quadrant : 4 * quadrant + 4, :]
+                    .rearrange("g r n -> r g n")
+                    .bitcast(I32),
+                )
+
         x_tiles = []
         for group in range(N_GROUPS):
+            if group == 1:
+                load_weight()
             x_sb = x_pool.tile([P, GROUP, K], BF16)
             x_tiles.append(x_sb)
             batch, first_row = divmod(group * GROUP, ROWS)

@@ -173,13 +173,17 @@ def tile_multiheadlatentattention_pb_t_kernel(tc, x, Wq_words, Wq_scales, out):
         nc.gpsimd.memset(cos_full[:, :, 0:NOPE_DIM], 1.0)
 
         quantised = {}
+        sums = {}
+        results = {}
+        by_head = [P, GROUP, HEADS, PAIRS, 2]
 
-        def regroup_and_quantise(group):
+        def regroup_and_quantise(group, quantise_after, between=None):
             x_sb = x_tiles[group]
             grouped = mx_pool.tile([P, GROUP, PASSES, P, 2], F32, align_bytes=64)
             codes = mx_pool.tile([P, GROUP, PASSES, P], U32, align_bytes=64)
             planes = mx_pool.tile([P, GROUP, PASSES, P], U8, align_bytes=64)
             quantised[group] = (codes, planes)
+            first = 0
             for t in range(GROUP):
                 words = x_sb[:, t, :].bitcast(F32)
                 xt = xt_pool.tile([P, PASSES, 2, P], F32)
@@ -191,19 +195,21 @@ def tile_multiheadlatentattention_pb_t_kernel(tc, x, Wq_words, Wq_scales, out):
                             identity[:],
                         )
                 nc.scalar.copy(out=grouped[:, t], in_=xt[:].rearrange("p g u n -> p g n u"))
-                if (t + 1) % QUANT_TILES == 0:
-                    done = slice(t + 1 - QUANT_TILES, t + 1)
+                if t + 1 in quantise_after:
+                    done = slice(first, t + 1)
                     nc.vector.quantize_mx(
                         out=codes[:, done].rearrange("p t g n -> p (t g n)").bitcast(FP8X4),
                         scales=planes[:, done].rearrange("p t g n -> p (t g n)"),
                         in_=grouped[:, done].rearrange("p t g n u -> p (t g n u)").bitcast(BF16),
                     )
+                    if first == 0 and between is not None:
+                        between()
+                    first = t + 1
 
-        def project_and_rotate(group):
+        def multiply(group):
             codes, planes = quantised[group]
-            batch, first_row = divmod(group * GROUP, ROWS)
-            rows = slice(first_row, first_row + GROUP)
             acc = acc_pool.tile([P, GROUP, HEADS, HEAD_DIM], F32)
+            sums[group] = acc
             for t in range(GROUP):
                 for g in range(PASSES):
                     nc.tensor.matmul_mx(
@@ -215,38 +221,52 @@ def tile_multiheadlatentattention_pb_t_kernel(tc, x, Wq_words, Wq_scales, out):
                         start=(g == 0),
                         stop=(g == PASSES - 1),
                     )
+
+        def rope_products(group, scalar_helps):
+            acc = sums[group]
+            first_row = (group * GROUP) % ROWS
+            rows = slice(first_row, first_row + GROUP)
             q_sb = q_pool.tile([P, GROUP, HEADS, HEAD_DIM], F32)
+            cross = cross_pool.tile(by_head, F32)
+            results[group] = (q_sb, cross)
+            kept = slice(NOPE_DIM, HEAD_DIM) if scalar_helps else slice(0, HEAD_DIM)
             nc.vector.tensor_tensor(
-                out=q_sb[:],
-                in0=acc[:],
-                in1=cos_full[:, rows, :].unsqueeze(2).to_broadcast([P, GROUP, HEADS, HEAD_DIM]),
+                out=q_sb[:, :, :, kept],
+                in0=acc[:, :, :, kept],
+                in1=cos_full[:, rows, kept]
+                .unsqueeze(2)
+                .to_broadcast([P, GROUP, HEADS, kept.stop - kept.start]),
                 op=ALU.mult,
             )
             pairs = acc[:, :, :, NOPE_DIM:HEAD_DIM].rearrange("p t h (i e) -> p t h i e", e=2)
-            cross = cross_pool.tile([P, 2, GROUP, HEADS, PAIRS], F32)
-            for place in range(2):
-                nc.vector.tensor_tensor(
-                    out=cross[:, place],
-                    in0=pairs[:, :, :, :, 1 - place],
-                    in1=sin_signed[:, place, rows, :]
-                    .unsqueeze(2)
-                    .to_broadcast([P, GROUP, HEADS, PAIRS]),
-                    op=ALU.mult,
-                )
-            rotated = q_sb[:, :, :, NOPE_DIM:HEAD_DIM].rearrange("p t h (i e) -> p t h i e", e=2)
             nc.vector.tensor_tensor(
+                out=cross[:],
+                in0=pairs[:, :, :, :, ::-1],
+                in1=sin_signed[:, rows].unsqueeze(2).to_broadcast(by_head),
+                op=ALU.mult,
+            )
+            if scalar_helps:
+                nc.scalar.copy(out=q_sb[:, :, :, 0:NOPE_DIM], in_=acc[:, :, :, 0:NOPE_DIM])
+
+        def rope_sum_and_store(group, engine):
+            q_sb, cross = results[group]
+            batch, first_row = divmod(group * GROUP, ROWS)
+            rotated = q_sb[:, :, :, NOPE_DIM:HEAD_DIM]
+            engine.tensor_tensor(
                 out=rotated,
                 in0=rotated,
-                in1=cross[:].rearrange("p e t h i -> p t h i e"),
+                in1=cross[:].rearrange("p t h i e -> p t h (i e)"),
                 op=ALU.add,
             )
-            nc.sync.dma_start(out=out_rows[batch, :, rows], in_=q_sb[:])
+            nc.sync.dma_start(out=out_rows[batch, :, first_row : first_row + GROUP], in_=q_sb[:])
 
-        regroup_and_quantise(0)
+        regroup_and_quantise(0, (2, 4))
 
-        sin_signed = keep.tile([P, 2, ROWS, PAIRS], F32)
-        nc.scalar.activation(out=sin_signed[:, 0], in_=sin_turns[:], func=SIN, scale=-math.pi)
-        nc.scalar.activation(out=sin_signed[:, 1], in_=sin_turns[:], func=SIN, scale=math.pi)
+        sin_signed = keep.tile([P, ROWS, PAIRS, 2], F32)
+        nc.scalar.activation(
+            out=sin_signed[:, :, :, 0], in_=sin_turns[:], func=SIN, scale=-math.pi
+        )
+        nc.scalar.activation(out=sin_signed[:, :, :, 1], in_=sin_turns[:], func=SIN, scale=math.pi)
         nc.scalar.activation(
             out=cos_full[:, :, NOPE_DIM:HEAD_DIM].rearrange("p j (i e) -> p j i e", e=2),
             in_=cos_turns[:].unsqueeze(3).to_broadcast([P, ROWS, PAIRS, 2]),
@@ -254,7 +274,16 @@ def tile_multiheadlatentattention_pb_t_kernel(tc, x, Wq_words, Wq_scales, out):
             scale=math.pi,
         )
 
+        LAST = N_GROUPS - 1
         for group in range(1, N_GROUPS):
-            regroup_and_quantise(group)
-            project_and_rotate(group - 1)
-        project_and_rotate(N_GROUPS - 1)
+            regroup_and_quantise(
+                group,
+                (2, 3, 4) if group == LAST else (2, 4),
+                (lambda c=group: rope_sum_and_store(c - 2, nc.vector)) if group >= 2 else None,
+            )
+            multiply(group - 1)
+            rope_products(group - 1, scalar_helps=(group == LAST))
+        rope_sum_and_store(LAST - 1, nc.gpsimd)
+        multiply(LAST)
+        rope_products(LAST, scalar_helps=True)
+        rope_sum_and_store(LAST, nc.vector)

@@ -30,7 +30,7 @@ ROWS = SEQ // P
 GROUP = 4
 GROUPS_PER_BATCH = ROWS // GROUP
 N_GROUPS = BATCH * GROUPS_PER_BATCH
-FINE_GROUPS = 6
+FINE_GROUPS = 16
 QUANT_TILES = 2
 
 ROUND_MAGIC = 1.5 * 2.0**23

@@ -32,6 +32,7 @@ GROUPS_PER_BATCH = ROWS // GROUP
 N_GROUPS = BATCH * GROUPS_PER_BATCH
 FINE_GROUPS = 16
 QUANT_TILES = 2
+SORT_FROM = 4
 
 ROUND_MAGIC = 1.5 * 2.0**23
 
@@ -126,6 +127,7 @@ def tile_multiheadlatentattention_pb_t_kernel(tc, x, Wq_words, Wq_scales, out):
         q_pool = ctx.enter_context(tc.tile_pool(name="q", bufs=N_GROUPS))
         mx_pool = ctx.enter_context(tc.tile_pool(name="mx", bufs=3))
         cross_pool = ctx.enter_context(tc.tile_pool(name="cross", bufs=2))
+        sorted_pool = ctx.enter_context(tc.tile_pool(name="sorted", bufs=4))
         xt_pool = ctx.enter_context(tc.psum_pool(name="xt", bufs=6))
         acc_pool = ctx.enter_context(tc.psum_pool(name="acc", bufs=2))
         ctx.enter_context(tc.manual_schedule())
@@ -176,6 +178,19 @@ def tile_multiheadlatentattention_pb_t_kernel(tc, x, Wq_words, Wq_scales, out):
         sums = {}
         results = {}
         by_head = [P, GROUP, HEADS, PAIRS, 2]
+        sorted_words = {}
+
+        def sort_words(group):
+            if group < SORT_FROM or group >= N_GROUPS:
+                return
+            in_order = sorted_pool.tile([P, PASSES, 2, P], F32)
+            nc.vector.tensor_copy(
+                out=in_order[:],
+                in_=x_tiles[group][:, 0, :]
+                .bitcast(F32)
+                .rearrange("n (g p u) -> n g u p", g=PASSES, u=2),
+            )
+            sorted_words[group] = in_order
 
         def regroup_and_quantise(group, quantise_after, between=None):
             x_sb = x_tiles[group]
@@ -189,11 +204,13 @@ def tile_multiheadlatentattention_pb_t_kernel(tc, x, Wq_words, Wq_scales, out):
                 xt = xt_pool.tile([P, PASSES, 2, P], F32)
                 for g in range(PASSES):
                     for u in range(2):
-                        nc.tensor.transpose(
-                            xt[:, g, u, :],
-                            words[:, WORDS_PER_PASS * g + u : WORDS_PER_PASS * (g + 1) : 2],
-                            identity[:],
-                        )
+                        if t == 0 and group in sorted_words:
+                            every_second = sorted_words[group][:, g, u, :]
+                        else:
+                            every_second = words[
+                                :, WORDS_PER_PASS * g + u : WORDS_PER_PASS * (g + 1) : 2
+                            ]
+                        nc.tensor.transpose(xt[:, g, u, :], every_second, identity[:])
                 nc.scalar.copy(out=grouped[:, t], in_=xt[:].rearrange("p g u n -> p g n u"))
                 if t + 1 in quantise_after:
                     done = slice(first, t + 1)
@@ -222,7 +239,8 @@ def tile_multiheadlatentattention_pb_t_kernel(tc, x, Wq_words, Wq_scales, out):
                         stop=(g == PASSES - 1),
                     )
 
-        def rope_products(group, scalar_helps):
+        def rope_products(group, scalar_first):
+            scalar_helps = True
             acc = sums[group]
             first_row = (group * GROUP) % ROWS
             rows = slice(first_row, first_row + GROUP)
@@ -230,6 +248,8 @@ def tile_multiheadlatentattention_pb_t_kernel(tc, x, Wq_words, Wq_scales, out):
             cross = cross_pool.tile(by_head, F32)
             results[group] = (q_sb, cross)
             kept = slice(NOPE_DIM, HEAD_DIM) if scalar_helps else slice(0, HEAD_DIM)
+            if scalar_first:
+                nc.scalar.copy(out=q_sb[:, :, :, 0:NOPE_DIM], in_=acc[:, :, :, 0:NOPE_DIM])
             nc.vector.tensor_tensor(
                 out=q_sb[:, :, :, kept],
                 in0=acc[:, :, :, kept],
@@ -245,7 +265,7 @@ def tile_multiheadlatentattention_pb_t_kernel(tc, x, Wq_words, Wq_scales, out):
                 in1=sin_signed[:, rows].unsqueeze(2).to_broadcast(by_head),
                 op=ALU.mult,
             )
-            if scalar_helps:
+            if not scalar_first:
                 nc.scalar.copy(out=q_sb[:, :, :, 0:NOPE_DIM], in_=acc[:, :, :, 0:NOPE_DIM])
 
         def rope_sum_and_store(group, engine):
@@ -282,8 +302,9 @@ def tile_multiheadlatentattention_pb_t_kernel(tc, x, Wq_words, Wq_scales, out):
                 (lambda c=group: rope_sum_and_store(c - 2, nc.vector)) if group >= 2 else None,
             )
             multiply(group - 1)
-            rope_products(group - 1, scalar_helps=(group == LAST))
+            rope_products(group - 1, scalar_first=(group != LAST))
+            sort_words(group + 2)
         rope_sum_and_store(LAST - 1, nc.gpsimd)
         multiply(LAST)
-        rope_products(LAST, scalar_helps=True)
+        rope_products(LAST, scalar_first=False)
         rope_sum_and_store(LAST, nc.vector)

@@ -171,8 +171,7 @@ def tile_multiheadlatentattention_pb_t_kernel(tc, x, Wq_words, Wq_scales, out):
         nc.scalar.activation(out=sin_warm[:], in_=sin_warm[:], func=SIN)
 
         sin_turns, cos_turns = rope_half_turns(nc, keep)
-        cos_full = keep.tile([P, ROWS, HEAD_DIM], F32)
-        nc.gpsimd.memset(cos_full[:, :, 0:NOPE_DIM], 1.0)
+        trig = keep.tile([P, 2, ROWS, HEADS, PAIRS, 2], F32)
 
         quantised = {}
         sums = {}
@@ -239,72 +238,67 @@ def tile_multiheadlatentattention_pb_t_kernel(tc, x, Wq_words, Wq_scales, out):
                         stop=(g == PASSES - 1),
                     )
 
-        def rope_products(group, scalar_first):
-            scalar_helps = True
+        def rope_products(group, nope_engine):
             acc = sums[group]
             first_row = (group * GROUP) % ROWS
             rows = slice(first_row, first_row + GROUP)
             q_sb = q_pool.tile([P, GROUP, HEADS, HEAD_DIM], F32)
-            cross = cross_pool.tile(by_head, F32)
-            results[group] = (q_sb, cross)
-            kept = slice(NOPE_DIM, HEAD_DIM) if scalar_helps else slice(0, HEAD_DIM)
-            if scalar_first:
-                nc.scalar.copy(out=q_sb[:, :, :, 0:NOPE_DIM], in_=acc[:, :, :, 0:NOPE_DIM])
-            nc.vector.tensor_tensor(
-                out=q_sb[:, :, :, kept],
-                in0=acc[:, :, :, kept],
-                in1=cos_full[:, rows, kept]
-                .unsqueeze(2)
-                .to_broadcast([P, GROUP, HEADS, kept.stop - kept.start]),
-                op=ALU.mult,
-            )
+            both = cross_pool.tile([P, 2] + by_head[1:], F32)
+            results[group] = (q_sb, both)
             pairs = acc[:, :, :, NOPE_DIM:HEAD_DIM].rearrange("p t h (i e) -> p t h i e", e=2)
+            if nope_engine == "scalar first":
+                nc.scalar.copy(out=q_sb[:, :, :, 0:NOPE_DIM], in_=acc[:, :, :, 0:NOPE_DIM])
             nc.vector.tensor_tensor(
-                out=cross[:],
-                in0=pairs[:, :, :, :, ::-1],
-                in1=sin_signed[:, rows].unsqueeze(2).to_broadcast(by_head),
+                out=both[:],
+                in0=pairs.unsqueeze(1).to_broadcast([P, 2] + by_head[1:]),
+                in1=trig[:, :, rows],
                 op=ALU.mult,
             )
-            if not scalar_first:
+            if nope_engine == "scalar":
                 nc.scalar.copy(out=q_sb[:, :, :, 0:NOPE_DIM], in_=acc[:, :, :, 0:NOPE_DIM])
+            if nope_engine == "vector":
+                nc.vector.tensor_copy(out=q_sb[:, :, :, 0:NOPE_DIM], in_=acc[:, :, :, 0:NOPE_DIM])
 
         def rope_sum_and_store(group, engine):
-            q_sb, cross = results[group]
+            q_sb, both = results[group]
             batch, first_row = divmod(group * GROUP, ROWS)
-            rotated = q_sb[:, :, :, NOPE_DIM:HEAD_DIM]
             engine.tensor_tensor(
-                out=rotated,
-                in0=rotated,
-                in1=cross[:].rearrange("p t h i e -> p t h (i e)"),
+                out=q_sb[:, :, :, NOPE_DIM:HEAD_DIM].rearrange("p t h (i e) -> p t h i e", e=2),
+                in0=both[:, 0],
+                in1=both[:, 1, :, :, :, ::-1],
                 op=ALU.add,
             )
             nc.sync.dma_start(out=out_rows[batch, :, first_row : first_row + GROUP], in_=q_sb[:])
 
         regroup_and_quantise(0, (2, 4))
 
-        sin_signed = keep.tile([P, ROWS, PAIRS, 2], F32)
         nc.scalar.activation(
-            out=sin_signed[:, :, :, 0], in_=sin_turns[:], func=SIN, scale=-math.pi
-        )
-        nc.scalar.activation(out=sin_signed[:, :, :, 1], in_=sin_turns[:], func=SIN, scale=math.pi)
-        nc.scalar.activation(
-            out=cos_full[:, :, NOPE_DIM:HEAD_DIM].rearrange("p j (i e) -> p j i e", e=2),
+            out=trig[:, 0, :, 0],
             in_=cos_turns[:].unsqueeze(3).to_broadcast([P, ROWS, PAIRS, 2]),
             func=SIN,
             scale=math.pi,
         )
+        nc.scalar.activation(
+            out=trig[:, 1, :, 0, :, 0], in_=sin_turns[:], func=SIN, scale=math.pi
+        )
+        nc.scalar.activation(
+            out=trig[:, 1, :, 0, :, 1], in_=sin_turns[:], func=SIN, scale=-math.pi
+        )
+        nc.vector.tensor_copy(
+            out=trig[:, :, :, 1].rearrange("p w j i e -> p w j (i e)"),
+            in_=trig[:, :, :, 0].rearrange("p w j i e -> p w j (i e)"),
+        )
 
         LAST = N_GROUPS - 1
         for group in range(1, N_GROUPS):
-            regroup_and_quantise(
-                group,
-                (2, 3, 4) if group == LAST else (2, 4),
-                (lambda c=group: rope_sum_and_store(c - 2, nc.vector)) if group >= 2 else None,
-            )
+            regroup_and_quantise(group, (2, 3, 4) if group == LAST else (2, 4))
             multiply(group - 1)
-            rope_products(group - 1, scalar_first=(group != LAST))
+            if group == LAST:
+                rope_products(group - 1, "scalar")
+            else:
+                rope_products(group - 1, "scalar first" if group % 2 else "vector")
             sort_words(group + 2)
-        rope_sum_and_store(LAST - 1, nc.gpsimd)
+            rope_sum_and_store(group - 1, nc.gpsimd if group == LAST else nc.vector)
         multiply(LAST)
-        rope_products(LAST, scalar_first=False)
+        rope_products(LAST, "scalar")
         rope_sum_and_store(LAST, nc.vector)

@@ -178,6 +178,7 @@ def tile_multiheadlatentattention_pb_t_kernel(tc, x, Wq_words, Wq_scales, out):
         results = {}
         by_head = [P, GROUP, HEADS, PAIRS, 2]
         sorted_words = {}
+        owed = []
 
         def sort_words(group):
             if group < SORT_FROM or group >= N_GROUPS:
@@ -221,6 +222,10 @@ def tile_multiheadlatentattention_pb_t_kernel(tc, x, Wq_words, Wq_scales, out):
                     if first == 0 and between is not None:
                         between()
                     first = t + 1
+            for earlier in owed:
+                copy_unrotated(nc.scalar.copy, earlier)
+                store(earlier)
+            owed.clear()
 
         def multiply(group):
             codes, planes = quantised[group]
@@ -238,6 +243,15 @@ def tile_multiheadlatentattention_pb_t_kernel(tc, x, Wq_words, Wq_scales, out):
                         stop=(g == PASSES - 1),
                     )
 
+        def copy_unrotated(copy, group):
+            copy(out=results[group][0][:, :, :, 0:NOPE_DIM], in_=sums[group][:, :, :, 0:NOPE_DIM])
+
+        def store(group):
+            batch, first_row = divmod(group * GROUP, ROWS)
+            nc.sync.dma_start(
+                out=out_rows[batch, :, first_row : first_row + GROUP], in_=results[group][0][:]
+            )
+
         def rope_products(group, nope_engine):
             acc = sums[group]
             first_row = (group * GROUP) % ROWS
@@ -246,8 +260,6 @@ def tile_multiheadlatentattention_pb_t_kernel(tc, x, Wq_words, Wq_scales, out):
             both = cross_pool.tile([P, 2] + by_head[1:], F32)
             results[group] = (q_sb, both)
             pairs = acc[:, :, :, NOPE_DIM:HEAD_DIM].rearrange("p t h (i e) -> p t h i e", e=2)
-            if nope_engine == "scalar first":
-                nc.scalar.copy(out=q_sb[:, :, :, 0:NOPE_DIM], in_=acc[:, :, :, 0:NOPE_DIM])
             nc.vector.tensor_tensor(
                 out=both[:],
                 in0=pairs.unsqueeze(1).to_broadcast([P, 2] + by_head[1:]),
@@ -255,20 +267,22 @@ def tile_multiheadlatentattention_pb_t_kernel(tc, x, Wq_words, Wq_scales, out):
                 op=ALU.mult,
             )
             if nope_engine == "scalar":
-                nc.scalar.copy(out=q_sb[:, :, :, 0:NOPE_DIM], in_=acc[:, :, :, 0:NOPE_DIM])
+                copy_unrotated(nc.scalar.copy, group)
             if nope_engine == "vector":
-                nc.vector.tensor_copy(out=q_sb[:, :, :, 0:NOPE_DIM], in_=acc[:, :, :, 0:NOPE_DIM])
+                copy_unrotated(nc.vector.tensor_copy, group)
+            if nope_engine == "scalar later":
+                owed.append(group)
 
         def rope_sum_and_store(group, engine):
             q_sb, both = results[group]
-            batch, first_row = divmod(group * GROUP, ROWS)
             engine.tensor_tensor(
                 out=q_sb[:, :, :, NOPE_DIM:HEAD_DIM].rearrange("p t h (i e) -> p t h i e", e=2),
                 in0=both[:, 0],
                 in1=both[:, 1, :, :, :, ::-1],
                 op=ALU.add,
             )
-            nc.sync.dma_start(out=out_rows[batch, :, first_row : first_row + GROUP], in_=q_sb[:])
+            if group not in owed:
+                store(group)
 
         regroup_and_quantise(0, (2, 4))
 
@@ -296,7 +310,7 @@ def tile_multiheadlatentattention_pb_t_kernel(tc, x, Wq_words, Wq_scales, out):
             if group == LAST:
                 rope_products(group - 1, "scalar")
             else:
-                rope_products(group - 1, "scalar first" if group % 2 else "vector")
+                rope_products(group - 1, "scalar later" if group % 2 else "vector")
             sort_words(group + 2)
             rope_sum_and_store(group - 1, nc.gpsimd if group == LAST else nc.vector)
         multiply(LAST)

import math
from contextlib import ExitStack

import concourse.mybir as mybir
from concourse.masks import make_identity

F32 = mybir.dt.float32
BF16 = mybir.dt.bfloat16
I32 = mybir.dt.int32
U32 = mybir.dt.uint32
U8 = mybir.dt.uint8
FP8X4 = mybir.dt.float8_e4m3fn_x4
FP4X4 = mybir.dt.float4_e2m1fn_x4
ALU = mybir.AluOpType
SIN = mybir.ActivationFunctionType.Sin

P = 128
BATCH, SEQ, K = 4, 2048, 1024
HEADS, HEAD_DIM, ROPE_DIM = 2, 64, 32
NOPE_DIM = HEAD_DIM - ROPE_DIM
PAIRS = ROPE_DIM // 2
N_OUT = HEADS * HEAD_DIM
ROPE_BASE = 10000.0

K_PASS = 4 * P
PASSES = K // K_PASS
WORDS_PER_PASS = K_PASS // 2

ROWS = SEQ // P
GROUP = 4
GROUPS_PER_BATCH = ROWS // GROUP
N_GROUPS = BATCH * GROUPS_PER_BATCH
FINE_GROUPS = 16
QUANT_TILES = 2
SORT_FROM = 4

ROUND_MAGIC = 1.5 * 2.0**23

FLOPS = 2 * BATCH * SEQ * K * N_OUT


def keep_bits(value, bits):
    if value == 0.0:
        return 0.0
    unit = 1.0
    while abs(value) / unit >= 2.0**bits:
        unit *= 2.0
    while abs(value) / unit < 2.0 ** (bits - 1):
        unit /= 2.0
    return round(value / unit) * unit


def rope_half_turns(nc, keep):
    table = [P, ROWS, PAIRS]

    rate = keep.tile([P, 2, PAIRS], F32)
    for i in range(PAIRS):
        exact = ROPE_BASE ** (-2.0 * i / ROPE_DIM) / math.pi
        high = keep_bits(exact, 24)
        nc.vector.memset(rate[:, 0, i : i + 1], high)
        nc.vector.memset(rate[:, 1, i : i + 1], keep_bits(exact - high, 24))

    position_int = keep.tile([P, ROWS], I32)
    nc.gpsimd.iota(position_int[:], pattern=[[1, ROWS]], base=0, channel_multiplier=ROWS)
    position = keep.tile([P, ROWS], F32)
    nc.vector.tensor_copy(out=position[:], in_=position_int[:])
    position_all_pairs = position[:].unsqueeze(2).to_broadcast(table)

    turns = keep.tile(table, F32)
    nc.vector.tensor_tensor(
        out=turns[:],
        in0=position_all_pairs,
        in1=rate[:, 0, :].unsqueeze(1).to_broadcast(table),
        op=ALU.mult,
    )
    turns_rest = keep.tile(table, F32)
    nc.vector.tensor_tensor(
        out=turns_rest[:],
        in0=position_all_pairs,
        in1=rate[:, 1, :].unsqueeze(1).to_broadcast(table),
        op=ALU.mult,
    )
    rounded = keep.tile(table, F32)
    nc.vector.tensor_scalar(
        out=rounded[:], in0=turns[:], scalar1=ROUND_MAGIC, scalar2=None, op0=ALU.add
    )
    odd = keep.tile(table, I32)
    nc.vector.tensor_scalar(
        out=odd[:], in0=rounded[:].bitcast(I32), scalar1=1, scalar2=None, op0=ALU.bitwise_and
    )
    minus_f = keep.tile(table, F32)
    nc.vector.scalar_tensor_tensor(
        out=minus_f[:],
        in0=rounded[:],
        scalar=ROUND_MAGIC,
        in1=turns[:],
        op0=ALU.subtract,
        op1=ALU.subtract,
    )
    sign = keep.tile(table, F32)
    nc.vector.tensor_scalar(
        out=sign[:], in0=odd[:], scalar1=-2.0, scalar2=1.0, op0=ALU.mult, op1=ALU.add
    )
    f = keep.tile(table, F32)
    nc.vector.tensor_tensor(out=f[:], in0=turns_rest[:], in1=minus_f[:], op=ALU.subtract)
    minus_abs_f = keep.tile(table, F32)
    nc.vector.scalar_tensor_tensor(
        out=minus_abs_f[:], in0=f[:], scalar=-1.0, in1=f[:], op0=ALU.mult, op1=ALU.min
    )
    sin_turns = keep.tile(table, F32)
    nc.vector.tensor_tensor(out=sin_turns[:], in0=f[:], in1=sign[:], op=ALU.mult)
    cos_turns = keep.tile(table, F32)
    nc.vector.scalar_tensor_tensor(
        out=cos_turns[:], in0=minus_abs_f[:], scalar=0.5, in1=sign[:], op0=ALU.add, op1=ALU.mult
    )
    return sin_turns, cos_turns


def tile_multiheadlatentattention_pb_t_kernel(tc, x, Wq_words, Wq_scales, out):
    nc = tc.nc
    x_rows = x.rearrange("b (p j) k -> b p j k", j=ROWS)
    out_rows = out.rearrange("b (p j) h d -> b p j h d", j=ROWS)

    with ExitStack() as ctx:
        keep = ctx.enter_context(tc.tile_pool(name="keep", bufs=1))
        x_pool = ctx.enter_context(tc.tile_pool(name="x", bufs=N_GROUPS))
        q_pool = ctx.enter_context(tc.tile_pool(name="q", bufs=N_GROUPS))
        mx_pool = ctx.enter_context(tc.tile_pool(name="mx", bufs=3))
        cross_pool = ctx.enter_context(tc.tile_pool(name="cross", bufs=2))
        sorted_pool = ctx.enter_context(tc.tile_pool(name="sorted", bufs=4))
        xt_pool = ctx.enter_context(tc.psum_pool(name="xt", bufs=6))
        acc_pool = ctx.enter_context(tc.psum_pool(name="acc", bufs=2))
        ctx.enter_context(tc.manual_schedule())

        w_planes = keep.tile([P, PASSES, N_OUT], U8, align_bytes=64)
        nc.vector.memset(w_planes[:].bitcast(I32), 0)
        sin_warm = keep.tile([P, 1], F32)
        nc.vector.memset(sin_warm[:], 0.0)
        identity = keep.tile([P, P], F32)
        make_identity(nc, identity[:])

        w_words = keep.tile([P, PASSES, 2 * N_OUT], U8, align_bytes=64)

        def load_weight():
            nc.sync.dma_start(
                out=w_words[:].bitcast(I32), in_=Wq_words.rearrange("g p b -> p g b").bitcast(I32)
            )
            for quadrant in range(4):
                nc.sync.dma_start(
                    out=w_planes[32 * quadrant : 32 * quadrant + 4].bitcast(I32),
                    in_=Wq_scales[:, 4 * quadrant : 4 * quadrant + 4, :]
                    .rearrange("g r n -> r g n")
                    .bitcast(I32),
                )

        x_tiles = []
        for group in range(N_GROUPS):
            if group == 1:
                load_weight()
            x_sb = x_pool.tile([P, GROUP, K], BF16)
            x_tiles.append(x_sb)
            batch, first_row = divmod(group * GROUP, ROWS)
            if group < FINE_GROUPS:
                for t in range(GROUP):
                    nc.sync.dma_start(out=x_sb[:, t, :], in_=x_rows[batch, :, first_row + t, :])
            else:
                nc.sync.dma_start(
                    out=x_sb[:], in_=x_rows[batch, :, first_row : first_row + GROUP, :]
                )

        nc.scalar.activation(out=sin_warm[:], in_=sin_warm[:], func=SIN)

        sin_turns, cos_turns = rope_half_turns(nc, keep)
        trig = keep.tile([P, 2, ROWS, HEADS, PAIRS, 2], F32)

        quantised = {}
        sums = {}
        results = {}
        by_head = [P, GROUP, HEADS, PAIRS, 2]
        sorted_words = {}
        owed = []

        def sort_words(group):
            if group < SORT_FROM or group >= N_GROUPS:
                return
            in_order = sorted_pool.tile([P, PASSES, 2, P], F32)
            nc.vector.tensor_copy(
                out=in_order[:],
                in_=x_tiles[group][:, 0, :]
                .bitcast(F32)
                .rearrange("n (g p u) -> n g u p", g=PASSES, u=2),
            )
            sorted_words[group] = in_order

        def regroup_and_quantise(group, quantise_after, between=None):
            x_sb = x_tiles[group]
            grouped = mx_pool.tile([P, GROUP, PASSES, P, 2], F32, align_bytes=64)
            codes = mx_pool.tile([P, GROUP, PASSES, P], U32, align_bytes=64)
            planes = mx_pool.tile([P, GROUP, PASSES, P], U8, align_bytes=64)
            quantised[group] = (codes, planes)
            first = 0
            for t in range(GROUP):
                words = x_sb[:, t, :].bitcast(F32)
                xt = xt_pool.tile([P, PASSES, 2, P], F32)
                for g in range(PASSES):
                    for u in range(2):
                        if t == 0 and group in sorted_words:
                            every_second = sorted_words[group][:, g, u, :]
                        else:
                            every_second = words[
                                :, WORDS_PER_PASS * g + u : WORDS_PER_PASS * (g + 1) : 2
                            ]
                        nc.tensor.transpose(xt[:, g, u, :], every_second, identity[:])
                nc.scalar.copy(out=grouped[:, t], in_=xt[:].rearrange("p g u n -> p g n u"))
                if t + 1 in quantise_after:
                    done = slice(first, t + 1)
                    nc.vector.quantize_mx(
                        out=codes[:, done].rearrange("p t g n -> p (t g n)").bitcast(FP8X4),
                        scales=planes[:, done].rearrange("p t g n -> p (t g n)"),
                        in_=grouped[:, done].rearrange("p t g n u -> p (t g n u)").bitcast(BF16),
                    )
                    if first == 0 and between is not None:
                        between()
                    first = t + 1
            for earlier in owed:
                copy_unrotated(nc.scalar.copy, earlier)
                store(earlier)
            owed.clear()

        def multiply(group):
            codes, planes = quantised[group]
            acc = acc_pool.tile([P, GROUP, HEADS, HEAD_DIM], F32)
            sums[group] = acc
            for t in range(GROUP):
                for g in range(PASSES):
                    nc.tensor.matmul_mx(
                        out=acc[:, t].rearrange("p h d -> p (h d)"),
                        lhsT=codes[:, t, g, :].bitcast(FP8X4),
                        lhsT_scale=planes[:, t, g, :],
                        rhs=w_words[:, g, :].bitcast(FP4X4),
                        rhs_scale=w_planes[:, g, :],
                        start=(g == 0),
                        stop=(g == PASSES - 1),
                    )

        def copy_unrotated(copy, group):
            copy(out=results[group][0][:, :, :, 0:NOPE_DIM], in_=sums[group][:, :, :, 0:NOPE_DIM])

        def store(group):
            batch, first_row = divmod(group * GROUP, ROWS)
            nc.sync.dma_start(
                out=out_rows[batch, :, first_row : first_row + GROUP], in_=results[group][0][:]
            )

        def rope_products(group, nope_engine):
            acc = sums[group]
            first_row = (group * GROUP) % ROWS
            rows = slice(first_row, first_row + GROUP)
            q_sb = q_pool.tile([P, GROUP, HEADS, HEAD_DIM], F32)
            both = cross_pool.tile([P, 2] + by_head[1:], F32)
            results[group] = (q_sb, both)
            pairs = acc[:, :, :, NOPE_DIM:HEAD_DIM].rearrange("p t h (i e) -> p t h i e", e=2)
            nc.vector.tensor_tensor(
                out=both[:],
                in0=pairs.unsqueeze(1).to_broadcast([P, 2] + by_head[1:]),
                in1=trig[:, :, rows],
                op=ALU.mult,
            )
            if nope_engine == "scalar":
                copy_unrotated(nc.scalar.copy, group)
            if nope_engine == "vector":
                copy_unrotated(nc.vector.tensor_copy, group)
            if nope_engine == "scalar later":
                owed.append(group)

        def rope_sum_and_store(group, engine):
            q_sb, both = results[group]
            engine.tensor_tensor(
                out=q_sb[:, :, :, NOPE_DIM:HEAD_DIM].rearrange("p t h (i e) -> p t h i e", e=2),
                in0=both[:, 0],
                in1=both[:, 1, :, :, :, ::-1],
                op=ALU.add,
            )
            if group not in owed:
                store(group)

        regroup_and_quantise(0, (2, 4))

        nc.scalar.activation(
            out=trig[:, 0, :, 0],
            in_=cos_turns[:].unsqueeze(3).to_broadcast([P, ROWS, PAIRS, 2]),
            func=SIN,
            scale=math.pi,
        )
        nc.scalar.activation(
            out=trig[:, 1, :, 0, :, 0], in_=sin_turns[:], func=SIN, scale=math.pi
        )
        nc.scalar.activation(
            out=trig[:, 1, :, 0, :, 1], in_=sin_turns[:], func=SIN, scale=-math.pi
        )
        nc.vector.tensor_copy(
            out=trig[:, :, :, 1].rearrange("p w j i e -> p w j (i e)"),
            in_=trig[:, :, :, 0].rearrange("p w j i e -> p w j (i e)"),
        )

        LAST = N_GROUPS - 1
        for group in range(1, N_GROUPS):
            regroup_and_quantise(group, (2, 3, 4) if group == LAST else (2, 4))
            multiply(group - 1)
            if group == LAST:
                rope_products(group - 1, "scalar")
            else:
                rope_products(group - 1, "scalar later" if group % 2 else "vector")
            sort_words(group + 2)
            rope_sum_and_store(group - 1, nc.gpsimd if group == LAST else nc.vector)
        multiply(LAST)
        rope_products(LAST, "scalar")
        rope_sum_and_store(LAST, nc.vector)
